import numpy as np
import ml_dtypes


def mxq(x, axis, fmt="e4m3"):
    dtype, down = {"e4m3": (ml_dtypes.float8_e4m3fn, 7), "e5m2": (ml_dtypes.float8_e5m2, 14)}[fmt]
    v = np.moveaxis(np.asarray(x, np.float32).astype(ml_dtypes.bfloat16).astype(np.float64), axis, -1)
    blocks = v.reshape(v.shape[:-1] + (-1, 32))
    amax = np.abs(blocks).max(-1, keepdims=True)
    byte = np.maximum(np.where(amax > 0, np.frexp(amax)[1] - 1 + 127, 0) - down, 1)
    scale = np.exp2(byte - 127.0)
    codes = (blocks / scale).astype(np.float32).astype(dtype).astype(np.float64)
    return np.moveaxis((codes * scale).reshape(v.shape), -1, axis)


WIDE = False


def mx_kscale(k):
    if not WIDE:
        return np.ones(k)
    levels = np.array([10, -10, 5, -5, 0])
    if k % 512:
        return np.exp2(np.random.permutation(np.resize(levels, k // 32))).repeat(32)
    a = np.empty((k // 512, 16))
    for p in range(k // 512):
        a[p, :8] = np.random.permutation(np.resize(levels, 8))
        for g in range(8):
            far = levels[np.abs(levels - a[p, g]) >= 10]
            a[p, g + 8] = far[np.random.randint(len(far))]
    return np.exp2(a.ravel()).repeat(32)


BF16 = ml_dtypes.bfloat16


def bf(x):
    return np.asarray(x, np.float32).astype(BF16)


def f64(x):
    return np.asarray(x).astype(np.float64)


E2M1 = np.array([0.0, 0.5, 1.0, 1.5, 2.0, 3.0, 4.0, 6.0, -0.0, -0.5, -1.0, -1.5, -2.0, -3.0, -4.0, -6.0])


def pack_weight(w, fmt):
    k, n = w.shape
    w = f64(bf(w)).reshape(k // 32, 32, n)
    amax = np.abs(w).max(1)
    if fmt == "e4m3":
        byte = np.frexp(amax)[1] - 1 + 127 - 7
    else:
        mant, ex = np.frexp(amax / 6.0)
        byte = np.where(mant > 0.5, ex, ex - 1) + 127
    byte = np.clip(np.where(amax > 0, byte, 1), 1, 254)
    scaled = (w * np.exp2(127.0 - byte)[:, None, :]).reshape(k, n).astype(np.float32)
    by_word = np.ascontiguousarray(scaled.reshape(k // 512, 128, 4, n).transpose(0, 1, 3, 2))
    if fmt == "e4m3":
        words = by_word.astype(ml_dtypes.float8_e4m3fn).view(np.uint8)
    else:
        c = by_word.astype(ml_dtypes.float4_e2m1fn).view(np.uint8) & 0xF
        words = c[..., 0::2] | (c[..., 1::2] << 4)
    return np.ascontiguousarray(words), np.ascontiguousarray(byte.astype(np.uint8).reshape(k // 512, 16, n))


def unpack_weight(words, scales, fmt):
    g, p, n, _ = words.shape
    if fmt == "e4m3":
        vals = np.ascontiguousarray(words).view(ml_dtypes.float8_e4m3fn).astype(np.float64)
    else:
        nib = np.empty((g, p, n, 4), np.uint8)
        nib[..., 0::2] = words & 0xF
        nib[..., 1::2] = words >> 4
        vals = E2M1[nib]
    vals = vals * np.repeat(np.exp2(scales.astype(np.float64) - 127.0), 8, axis=1)[..., None]
    return vals.transpose(0, 1, 3, 2).reshape(g * 512, n)


B, C, NH, GW, GH, GZ = 2, 1024, 2, 16, 8, 8
N = GW * GH * GZ
D = C // NH
XS = 2.0


def draw0():
    s, t = mx_kscale(C), mx_kscale(D)
    g = np.random.standard_normal((B, NH, D, D)) * np.sqrt(1.0 + C / N)
    e = np.exp(g - g.max(-1, keepdims=True))
    attn = e / e.sum(-1, keepdims=True)
    x = bf(XS * np.random.standard_normal((B, C, GW, GH, GZ)) * s[None, :, None, None, None])
    words, scales = pack_weight(np.random.standard_normal((C, C)) / np.sqrt(C) / s[:, None] * np.tile(t, NH)[None, :], "e4m3")
    return {"x": x,
            "w_v_words": words,
            "w_v_scales": scales,
            "attn": bf(attn / t)}


def core(x, w_v_words, w_v_scales, attn):
    xt = f64(x).reshape(B, C, N).transpose(0, 2, 1)
    v = mxq(xt, 2, "e4m3") @ unpack_weight(w_v_words, w_v_scales, "e4m3")
    v = v.reshape(B, N, NH, D).transpose(0, 2, 3, 1)
    out = mxq(f64(attn), 3, "e4m3") @ mxq(v, 2, "e4m3")
    out = out.transpose(0, 3, 1, 2).reshape(B, N, C)
    return out.reshape(B, GW, GH, GZ, C).transpose(0, 4, 1, 2, 3)


def e4m3fn_bytes(y):
    return np.clip(np.asarray(y, np.float64), -448.0, 448.0).astype(np.float32).astype(ml_dtypes.float8_e4m3fn).view(np.uint8)


def e4m3fn_values(b):
    return np.asarray(b, np.uint8).view(ml_dtypes.float8_e4m3fn).astype(np.float64)


def setup_inputs():
    d = draw0()
    x0 = np.asarray(d['x']).astype(np.float64)
    s = (np.max(np.abs(x0), axis=(0, 2, 3, 4), keepdims=True) / 448.0).astype(np.float32)
    out = {}
    for k, v in d.items():
        if k == 'x':
            out['x_bytes'] = e4m3fn_bytes(x0 / s.astype(np.float64))
            out['x_scale'] = s
        else:
            out[k] = v
    return out


def reference(x_bytes, x_scale, w_v_words, w_v_scales, attn):
    return core(e4m3fn_values(x_bytes) * x_scale.astype(np.float64), w_v_words, w_v_scales, attn)

from contextlib import ExitStack

import concourse.mybir as mybir
from concourse.masks import make_identity

F32 = mybir.dt.float32
BF16 = mybir.dt.bfloat16
I32 = mybir.dt.int32
U32 = mybir.dt.uint32
U8 = mybir.dt.uint8
FP8 = mybir.dt.float8_e4m3fn
FP8X4 = mybir.dt.float8_e4m3fn_x4
COPY = mybir.ActivationFunctionType.Copy
MULT = mybir.AluOpType.mult

B = 2
C = 1024
N = 1024
H = 2
D = 512
P = 128
T = 4
G = 2
SUB = 128
BANK = 512

FLOPS = 2 * B * C * C * N + 2 * B * H * D * D * N

X_LOADS = [(0, 0, 512), (0, 512, 512), (1, 0, 1024)]
WIDENS = [(0, 0, 256), (0, 256, 256), (0, 512, 512), (1, 0, 512), (1, 512, 512)]
CHUNKS = [(0, 0, 256), (0, 256, 256), (0, 512, 512)] + [(1, n0, 256) for n0 in range(0, N, 256)]
WMAX = max(width for b, n0, width in CHUNKS)
ORDER = ["ws", "x0", "a00", "w0", "w1", "a01", "x1", "x2", "a10", "a11"]

V_BANKS, OUT_BANKS, ATTN_BANKS = 4, 3, 1
V_TILES = 4
STAGES = 12

START = 840.0
FIRST_LOAD = 3600.0
LOAD_BYTES = 510.0
HOP = 350.0
SAME_ENGINE = 72.0
QUANTIZE_HOP = 180.0
FIXED = 30
SCALE_TILE = 50.0
WIDEN = {"vector": 0.5, "scalar": 0.81}
INTERLEAVE = 0.62
QUANTIZE = 0.26
PERMUTE = 900.0
STAGE1_PASSES = 570.0
STAGE2_PASSES = 266.0
TRANSPOSES = 504.0
SCALAR_WIDENS = 3
SPLIT_QUANTIZE = 1
PREFETCH = 512
LEAD = 1000.0
LATE_WAIT = 2400.0
EARLY_WAIT = 1000.0
WINDOW = {"vector": 50.0, "scalar": 80.0, "tensor": 60.0}
OUT_LATE = 500.0
ATTN_AFTER = (2, 2, 12, 16)
FIRST_RANK = 0
DUE_RANK = 0.8
BANK_RANK = 1
PREPARE_RANK = 2
LATER_RANK = 2.5
SPARE_RANK = 5


def locate(ranges, b, n):
    for i, (rb, n0, width) in enumerate(ranges):
        if rb == b and n0 <= n < n0 + width:
            return i, n - n0
    raise ValueError("no range holds this voxel")


def tile_channelattention_pb_w8_kernel(tc, x_bytes, x_scale, w_v_words, w_v_scales, attn, out):
    nc = tc.nc
    x_hbm = x_bytes.rearrange("b (g p t) w y z -> b g p t (w y z)", p=P, t=T)
    scale_hbm = x_scale.rearrange("o (g p t) w y z -> p (o g) (t w y z)", p=P, t=T)
    attn_hbm = attn.rearrange("b h (r i) j -> b h r i j", i=T)
    out_hbm = out.rearrange("b (h r i) w y z -> b h r i (w y z)", h=H, i=T)

    with ExitStack() as ctx:
        keep = ctx.enter_context(tc.tile_pool(name="keep", bufs=1))
        work = ctx.enter_context(tc.tile_pool(name="work", bufs=2))
        psum = ctx.enter_context(tc.psum_pool(name="psum", bufs=1))

        def kept(name, shape, dtype):
            return keep.tile(shape, dtype, name=name, align_bytes=64)

        identity = kept("identity", [P, P], F32)
        make_identity(nc, identity[:])
        warm_in = kept("warm_in", [P, 1], F32)
        warm_out = kept("warm_out", [P, 1], F32)
        nc.vector.memset(warm_in[:], 0.0)

        heads = [(b, h) for b in range(B) for h in range(H)]
        x_scales = kept("x_scales", [P, G, T], F32)
        x_raw = [kept(f"x_raw{i}", [P, G, T, width], U8) for i, (b, n0, width) in enumerate(X_LOADS)]
        x_wide = [[kept(f"x_wide{q}_{g}", [P, T, width], BF16) for g in range(G)] for q, (b, n0, width) in enumerate(WIDENS)]
        x_grouped = [kept(f"x_grouped{c}", [P, G, width, T], BF16) for c, (b, n0, width) in enumerate(CHUNKS)]
        x_codes = [kept(f"x_codes{c}", [P, G, width], U32) for c, (b, n0, width) in enumerate(CHUNKS)]
        x_planes = [kept(f"x_planes{c}", [P, G, width], U8) for c, (b, n0, width) in enumerate(CHUNKS)]
        w_raw = [kept(f"w_raw{h}", [P, G, D], I32) for h in range(H)]
        w_codes = [kept(f"w_codes{h}", [P, G, T, P], I32) for h in range(H)]
        w_planes_raw = kept("w_planes_raw", [P, C], U8)
        w_planes = [kept(f"w_planes{h}", [P, T, P], U8) for h in range(H)]
        attn_raw = {(b, h): kept(f"attn_raw{b}{h}", [P, T, D], BF16) for b, h in heads}
        attn_grouped = {(b, h): kept(f"attn_grouped{b}{h}", [P, D, T], BF16) for b, h in heads}
        attn_codes = {(b, h): kept(f"attn_codes{b}{h}", [P, D], U32) for b, h in heads}
        attn_planes = {(b, h): kept(f"attn_planes{b}{h}", [P, D], U8) for b, h in heads}

        nc.vector.memset(w_planes_raw[:].bitcast(I32), 0)

        copy_on = {"vector": nc.vector.tensor_copy, "scalar": nc.scalar.copy}


        def load(name):
            if name == "ws":
                for q in range(4):
                    nc.sync.dma_start(
                        out=w_planes_raw[32 * q : 32 * q + 4 * G, :].bitcast(I32),
                        in_=w_v_scales[:, 4 * q : 4 * q + 4, :].bitcast(I32),
                    )
                return G * 16 * C
            if name[0] == "x":
                i = int(name[1])
                b, n0, width = X_LOADS[i]
                for g in range(G):
                    nc.sync.dma_start(out=x_raw[i][:, g, :, :], in_=x_hbm[b, g][:, :, n0 : n0 + width])
                return C * width * (N / width) ** 0.5
            if name[0] == "w":
                h = int(name[1])
                for g in range(G):
                    nc.sync.dma_start(
                        out=w_raw[h][:, g, :],
                        in_=w_v_words[g].rearrange("p n t -> p (n t)")[:, h * D * T : (h + 1) * D * T].bitcast(I32),
                    )
                return C * D
            b, h = int(name[1]), int(name[2])
            nc.sync.dma_start(out=attn_raw[b, h][:], in_=attn_hbm[b, h])
            return 2 * D * D

        def permute_w(h):
            nc.vector.tensor_copy(out=w_codes[h][:].rearrange("p g t m -> p g m t"), in_=w_raw[h][:].rearrange("p g (m t) -> p g m t", t=T))
            nc.vector.tensor_copy(
                out=w_planes[h][:].rearrange("p t m -> p m t"),
                in_=w_planes_raw[:, h * D : (h + 1) * D].rearrange("p (m t) -> p m t", t=T),
            )

        def widen(engine, q, g, t):
            b, n0, width = WIDENS[q]
            i, first = locate(X_LOADS, b, n0)
            source = x_raw[i][:, g, t, first : first + width].bitcast(FP8)
            factor = x_scales[:, g, t : t + 1]
            if engine == "scalar":
                nc.scalar.activation(out=x_wide[q][g][:, t, :], in_=source, func=COPY, scale=factor)
            else:
                nc.vector.tensor_scalar(out=x_wide[q][g][:, t, :], in0=source, scalar1=factor, scalar2=None, op0=MULT)

        def interleave_x(c, g):
            b, n0, width = CHUNKS[c]
            q, first = locate(WIDENS, b, n0)
            nc.vector.tensor_copy(
                out=x_grouped[c][:, g].rearrange("p (s i) t -> p s t i", i=4),
                in_=x_wide[q][g][:, :, first : first + width].rearrange("p t (s i) -> p s t i", i=4),
            )

        def quantize_x(c, g):
            nc.vector.quantize_mx(
                out=x_codes[c][:, g, :].bitcast(FP8X4), scales=x_planes[c][:, g, :], in_=x_grouped[c][:, g].rearrange("p n t -> p (n t)")
            )

        def quantize_x_both(c):
            nc.vector.quantize_mx(
                out=x_codes[c][:].rearrange("p g n -> p (g n)").bitcast(FP8X4),
                scales=x_planes[c][:].rearrange("p g n -> p (g n)"),
                in_=x_grouped[c][:].rearrange("p g n t -> p (g n t)"),
            )

        def multiply_v(c, h, first):
            bank = psum.tile([P, T, SUB], F32, name="v_bank", tag="v_bank", bufs=V_BANKS)
            for t in range(T):
                for g in range(G):
                    nc.tensor.matmul_mx(
                        out=bank[:, t, :],
                        lhsT=w_codes[h][:, g, t, :].bitcast(FP8X4),
                        lhsT_scale=w_planes[h][4 * g : P, t, :],
                        rhs=x_codes[c][:, g, first : first + SUB].bitcast(FP8X4),
                        rhs_scale=x_planes[c][:, g, first : first + SUB],
                        start=(g == 0),
                        stop=(g == G - 1),
                    )
            return bank

        v_grouped = {}
        v_codes = {}
        v_planes = {}

        def empty_v(engine, c, h, first, bank):
            if first == 0:
                v_grouped[c, h] = work.tile([P, WMAX, T], BF16, name="v_grouped", tag="v_grouped", bufs=V_TILES, align_bytes=64)
            copy_on[engine](out=v_grouped[c, h][:, first : first + SUB, :], in_=bank[:].rearrange("p t n -> p n t"))

        def quantize_v(c, h):
            width = CHUNKS[c][2]
            v_codes[c, h] = work.tile([P, WMAX], U32, name="v_codes", tag="v_codes", bufs=V_TILES, align_bytes=64)
            v_planes[c, h] = work.tile([P, WMAX], U8, name="v_planes", tag="v_planes", bufs=V_TILES, align_bytes=64)
            nc.vector.quantize_mx(
                out=v_codes[c, h][:, 0:width].bitcast(FP8X4),
                scales=v_planes[c, h][:, 0:width],
                in_=v_grouped[c, h][:, 0:width, :].rearrange("p n t -> p (n t)"),
            )

        def transpose_attn(b, h, pair):
            words = attn_raw[b, h][:].rearrange("r i j -> r (i j)").bitcast(F32)
            bank = psum.tile([P, 2, 2, P], F32, name="attn_bank", tag="attn_bank", bufs=ATTN_BANKS)
            for i in range(2):
                first = (2 * pair + i) * (D // 2)
                for u in range(2):
                    nc.tensor.transpose(bank[:, i, u, :], words[:, first + u : first + D // 2 : 2], identity[:])
            return bank

        def empty_attn(engine, b, h, pair, bank):
            words = attn_grouped[b, h][:].rearrange("p i t -> p (i t)").bitcast(F32)
            copy_on[engine](
                out=words[:, pair * BANK : (pair + 1) * BANK].rearrange("p (i r u) -> p i r u", i=2, u=2),
                in_=bank[:].rearrange("p i u r -> p i r u"),
            )

        def quantize_attn(b, h):
            nc.vector.quantize_mx(
                out=attn_codes[b, h][:].bitcast(FP8X4), scales=attn_planes[b, h][:], in_=attn_grouped[b, h][:].rearrange("p i t -> p (i t)")
            )

        def multiply_out(c, h, i0):
            b, n0, width = CHUNKS[c]
            bank = psum.tile([P, BANK // width, width], F32, name="out_bank", tag="out_bank", bufs=OUT_BANKS)
            for k in range(BANK // width):
                rows = slice((i0 + k) * P, (i0 + k + 1) * P)
                nc.tensor.matmul_mx(
                    out=bank[:, k, :],
                    lhsT=attn_codes[b, h][:, rows].bitcast(FP8X4),
                    lhsT_scale=attn_planes[b, h][:, rows],
                    rhs=v_codes[c, h][:, 0:width].bitcast(FP8X4),
                    rhs_scale=v_planes[c, h][:, 0:width],
                    start=True,
                    stop=True,
                )
            return bank

        def empty_out(engine, c, h, i0, bank):
            b, n0, width = CHUNKS[c]
            stage = work.tile([P, BANK // width, width], F32, name="stage", tag="stage", bufs=STAGES)
            copy_on[engine](out=stage[:], in_=bank[:])
            nc.sync.dma_start(out=out_hbm[b, h][:, i0 : i0 + BANK // width, n0 : n0 + width], in_=stage[:])

        jobs = []
        clock = {"vector": START, "scalar": START, "tensor": START}
        free_banks = {"v": [0.0] * V_BANKS, "out": [0.0] * OUT_BANKS, "attn": [0.0] * ATTN_BANKS}
        progress = {"quantised": 0, "stage1": 0}
        landed = {}

        def offer(engines, ready, cost, rank, emit, done=None, takes=None, frees=None):
            costs = cost if isinstance(cost, dict) else {engine: cost for engine in engines}
            jobs.append(dict(costs=costs, ready=ready, rank=rank, emit=emit, done=done, takes=takes, frees=frees))

        def offer_copy(end, rank, emit, done, tag):
            offer(("vector", "scalar"), end + HOP, FIXED + BANK, rank, emit, done, frees=tag)

        banks = {}
        w_ready = {}
        x_ready = {}
        v_ready = {}
        attn_ready = {}
        ends = {}

        def gather(key, count, end):
            ends.setdefault(key, []).append(end)
            return max(ends[key]) if len(ends[key]) == count else None

        def offer_permute(h):
            def done(end):
                w_ready[h] = end
                offer_stage1()

            offer(("vector",), landed[f"w{h}"], PERMUTE, (PREPARE_RANK if h == 0 else LATER_RANK, -1), lambda engine: permute_w(h), done)

        opened = []

        def open_widens():
            for q, (b, n0, width) in enumerate(WIDENS):
                if q not in opened and N * b + n0 <= progress["quantised"] + PREFETCH:
                    opened.append(q)
                    offer_widens(q)

        def offer_widens(q):
            b, n0, width = WIDENS[q]
            i = locate(X_LOADS, b, n0)[0]
            c0 = locate(CHUNKS, b, n0)[0]
            inside = [c for c, (cb, cn, cw) in enumerate(CHUNKS) if cb == b and n0 <= cn < n0 + width]
            for g in range(G):
                for t in range(T):

                    def done(end, g=g):
                        last = gather(("wide", q, g), T, end)
                        if last is not None:
                            for c in inside:
                                offer_interleave(c, g, last)

                    engines = ("vector", "scalar") if q < SCALAR_WIDENS else ("vector",)
                    cost = {engine: FIXED + SCALE_TILE + WIDEN[engine] * width for engine in engines}
                    offer(engines, landed[f"x{i}"], cost, (PREPARE_RANK, c0, g, 0, t), lambda engine, g=g, t=t: widen(engine, q, g, t), done)

        def offer_interleave(c, g, ready):
            width = CHUNKS[c][2]

            def done(end):
                if c < SPLIT_QUANTIZE:
                    offer_quantize(end, 1, (PREPARE_RANK, c, g, 2), lambda engine: quantize_x(c, g), lambda last: quantised(gather(("x", c), G, last)))
                else:
                    if gather(("grouped", c), G, end) is not None:
                        offer_quantize(end, G, (PREPARE_RANK, c, G - 1, 2), lambda engine: quantize_x_both(c), quantised)

            def offer_quantize(end, passes, rank, emit, after):
                offer(("vector",), end + QUANTIZE_HOP, FIXED + QUANTIZE * width * T * passes, rank, emit, after)

            def quantised(end):
                if end is not None:
                    x_ready[c] = end
                    progress["quantised"] += width
                    open_widens()
                    offer_stage1()

            offer(("vector",), ready + SAME_ENGINE, FIXED + INTERLEAVE * width * T, (PREPARE_RANK, c, g, 1), lambda engine: interleave_x(c, g), done)

        waiting = [(c, h, n) for c, (b, n0, width) in enumerate(CHUNKS) for h in range(H) for n in range(0, width, SUB)]
        number = {item: s for s, item in enumerate(waiting)}

        def offer_stage1():
            while waiting and waiting[0][0] in x_ready and waiting[0][1] in w_ready:
                c, h, n = waiting.pop(0)

                def emit(engine, c=c, h=h, n=n):
                    banks["v_bank", c, h, n] = multiply_v(c, h, n)

                def copied(end, c=c, h=h, n=n):
                    width = CHUNKS[c][2]
                    last = gather(("v", c, h), width // SUB, end)
                    if last is not None:
                        offer(("vector",), last + HOP, FIXED + QUANTIZE * T * width, (FIRST_RANK, number[c, h, n]), lambda engine: quantize_v(c, h), lambda q_end: quantised_v(c, h, q_end))

                def done(end, c=c, h=h, n=n, copied=copied):
                    progress["stage1"] += 1
                    offer_copy(end, (BANK_RANK, end), lambda engine: empty_v(engine, c, h, n, banks["v_bank", c, h, n]), copied, "v")

                offer(("tensor",), max(x_ready[c], w_ready[h]) + HOP, STAGE1_PASSES, (BANK_RANK, number[c, h, n]), emit, done, takes="v")

        def quantised_v(c, h, end):
            v_ready[c, h] = end
            offer_stage2(c, h)

        def offer_stage2(c, h):
            b, n0, width = CHUNKS[c]
            if (c, h) not in v_ready or (b, h) not in attn_ready:
                return
            for i0 in range(0, T, BANK // width):

                def emit(engine, i0=i0):
                    banks["out_bank", c, h, i0] = multiply_out(c, h, i0)

                def done(end, i0=i0):
                    offer_copy(end, (BANK_RANK, end + OUT_LATE), lambda engine: empty_out(engine, c, h, i0, banks["out_bank", c, h, i0]), None, "out")

                offer(("tensor",), max(v_ready[c, h], attn_ready[b, h]) + HOP, STAGE2_PASSES, (FIRST_RANK, c, h, i0), emit, done, takes="out")

        def offer_attn(b, h):
            def quantised_attn(end):
                attn_ready[b, h] = end
                for c in range(len(CHUNKS)):
                    if CHUNKS[c][0] == b:
                        offer_stage2(c, h)

            def copied(end):
                last = gather(("attn", b, h), 2, end)
                if last is not None:
                    offer(("vector",), last + HOP, FIXED + QUANTIZE * D * T, (FIRST_RANK, 0), lambda engine: quantize_attn(b, h), quantised_attn)

            for pair in range(2):

                def emit(engine, pair=pair):
                    banks["attn_bank", b, h, pair] = transpose_attn(b, h, pair)

                def done(end, pair=pair):
                    offer_copy(end, (BANK_RANK, end), lambda engine: empty_attn(engine, b, h, pair, banks["attn_bank", b, h, pair]), copied, "attn")

                offer(("tensor",), landed[f"a{b}{h}"], TRANSPOSES, (BANK_RANK, ATTN_AFTER[H * b + h], pair), emit, done, takes="attn")

        def candidate(engine):
            late = progress["quantised"] - progress["stage1"] * SUB / H < LEAD and progress["quantised"] < B * N
            found = []
            for job in jobs:
                if engine not in job["costs"] or (job["takes"] and not free_banks[job["takes"]]):
                    continue
                start = max(clock[engine], job["ready"])
                if job["takes"]:
                    start = max(start, min(free_banks[job["takes"]]) + HOP)
                rank = job["rank"]
                if engine == "vector" and job["frees"]:
                    backlog = sum(1 for other in jobs if other["frees"] and other["ready"] <= start)
                    wait = clock["scalar"] + (FIXED + BANK) * (backlog - 1) - start
                    rank = (DUE_RANK if wait > (LATE_WAIT if late else EARLY_WAIT) else SPARE_RANK,) + rank
                found.append((start, rank, job))
            if not found:
                return None
            limit = min(start for start, rank, job in found) + WINDOW[engine]
            start, rank, job = min((f for f in found if f[0] <= limit), key=lambda f: (f[1], f[0]))
            return start, job

        def run():
            while jobs:
                picks = [(engine, candidate(engine)) for engine in clock]
                engine, (start, job) = min((p for p in picks if p[1]), key=lambda p: p[1][0])
                jobs.remove(job)
                job["emit"](engine)
                end = start + job["costs"][engine]
                clock[engine] = end
                if job["takes"]:
                    free_banks[job["takes"]].remove(min(free_banks[job["takes"]]))
                if job["frees"]:
                    free_banks[job["frees"]].append(end)
                if job["done"]:
                    job["done"](end)

        with tc.manual_schedule():
            nc.scalar.dma_start(out=x_scales[:], in_=scale_hbm)
            nc.scalar.activation(out=warm_out[:], in_=warm_in[:], func=COPY)
            moved = 0
            for name in ORDER:
                moved += load(name)
                landed[name] = FIRST_LOAD + moved / LOAD_BYTES
            open_widens()
            for h in range(H):
                offer_permute(h)
            for b, h in heads:
                offer_attn(b, h)
            run()
